import numpy as np
import ml_dtypes


def mxq(x, axis, fmt="e4m3"):
    dtype, down = {"e4m3": (ml_dtypes.float8_e4m3fn, 7), "e5m2": (ml_dtypes.float8_e5m2, 14)}[fmt]
    v = np.moveaxis(np.asarray(x, np.float32).astype(ml_dtypes.bfloat16).astype(np.float64), axis, -1)
    blocks = v.reshape(v.shape[:-1] + (-1, 32))
    amax = np.abs(blocks).max(-1, keepdims=True)
    byte = np.maximum(np.where(amax > 0, np.frexp(amax)[1] - 1 + 127, 0) - down, 1)
    scale = np.exp2(byte - 127.0)
    codes = (blocks / scale).astype(np.float32).astype(dtype).astype(np.float64)
    return np.moveaxis((codes * scale).reshape(v.shape), -1, axis)


WIDE = False


def mx_kscale(k):
    if not WIDE:
        return np.ones(k)
    levels = np.array([10, -10, 5, -5, 0])
    a = np.random.permutation(np.resize(levels, k // 512 * 4)).reshape(k // 512, 4)
    idx = np.arange(k)
    return np.exp2(a[idx // 512, idx % 128 // 32])


BF16 = ml_dtypes.bfloat16


def bf(x):
    return np.asarray(x, np.float32).astype(BF16)


def f64(x):
    return np.asarray(x).astype(np.float64)


E2M1 = np.array([0.0, 0.5, 1.0, 1.5, 2.0, 3.0, 4.0, 6.0, -0.0, -0.5, -1.0, -1.5, -2.0, -3.0, -4.0, -6.0])


def pack_weight(w, fmt):
    k, n = w.shape
    w = f64(bf(w)).reshape(k // 32, 32, n)
    amax = np.abs(w).max(1)
    if fmt == "e4m3":
        byte = np.frexp(amax)[1] - 1 + 127 - 7
    else:
        mant, ex = np.frexp(amax / 6.0)
        byte = np.where(mant > 0.5, ex, ex - 1) + 127
    byte = np.clip(np.where(amax > 0, byte, 1), 1, 254)
    scaled = (w * np.exp2(127.0 - byte)[:, None, :]).reshape(k, n).astype(np.float32)
    by_word = np.ascontiguousarray(scaled.reshape(k // 512, 128, 4, n).transpose(0, 1, 3, 2))
    if fmt == "e4m3":
        words = by_word.astype(ml_dtypes.float8_e4m3fn).view(np.uint8)
    else:
        c = by_word.astype(ml_dtypes.float4_e2m1fn).view(np.uint8) & 0xF
        words = c[..., 0::2] | (c[..., 1::2] << 4)
    return np.ascontiguousarray(words), np.ascontiguousarray(byte.astype(np.uint8).reshape(k // 512, 16, n))


def unpack_weight(words, scales, fmt):
    g, p, n, _ = words.shape
    if fmt == "e4m3":
        vals = np.ascontiguousarray(words).view(ml_dtypes.float8_e4m3fn).astype(np.float64)
    else:
        nib = np.empty((g, p, n, 4), np.uint8)
        nib[..., 0::2] = words & 0xF
        nib[..., 1::2] = words >> 4
        vals = E2M1[nib]
    vals = vals * np.repeat(np.exp2(scales.astype(np.float64) - 127.0), 8, axis=1)[..., None]
    return vals.transpose(0, 1, 3, 2).reshape(g * 512, n)

def pack4(w):
    words, scales = pack_weight(w, "e2m1")
    return words.reshape(words.shape[0], 128, -1), scales


def unpack4(words, scales):
    return unpack_weight(words.reshape(words.shape[0], 128, -1, 2), scales, "e2m1")


B, S, D, DM, DK = 4, 1024, 512, 1024, 64
LN_EPS = 1e-5


def setup_inputs():
    s = mx_kscale(DM)
    h_attn = bf(np.random.standard_normal((B, S, DM)) * 0.3 * s)
    Wo_words, Wo_scales = pack4(np.random.standard_normal((DM, D)) * 3.0 / np.sqrt(DM) / s[:, None])
    return {
        "h_attn": h_attn,
        "Wo_words": Wo_words,
        "Wo_scales": Wo_scales,
        "bo": bf(np.random.standard_normal((B, S, D)) * 0.5 + np.random.uniform(0.25, 0.75, (B, 1, 1))),
        "x": bf(np.random.standard_normal((B, S, D))),
        "gamma": bf(1.0 + 0.1 * np.random.standard_normal((S, D))),
        "beta": bf(0.1 * np.random.standard_normal((S, D))),
    }


def reference(h_attn, Wo_words, Wo_scales, bo, x, gamma, beta):
    o = (mxq(f64(h_attn), 2, "e4m3") @ unpack4(Wo_words, Wo_scales)) + f64(bo)
    o = o + f64(x)
    mu = o.mean(axis=(-2, -1), keepdims=True)
    var = np.square(o - mu).mean(axis=(-2, -1), keepdims=True)
    return (o - mu) / np.sqrt(var + LN_EPS) * f64(gamma) + f64(beta)

@@ -1,0 +1,263 @@
+from contextlib import ExitStack
+
+import concourse.mybir as mybir
+from concourse.masks import make_identity
+
+F32 = mybir.dt.float32
+BF16 = mybir.dt.bfloat16
+I32 = mybir.dt.int32
+U32 = mybir.dt.uint32
+U8 = mybir.dt.uint8
+FP8X4 = mybir.dt.float8_e4m3fn_x4
+FP4X4 = mybir.dt.float4_e2m1fn_x4
+ALU = mybir.AluOpType
+ACT = mybir.ActivationFunctionType
+
+P = 128
+BATCH, SEQ, D_MODEL, D_OUT = 4, 1024, 1024, 512
+LN_EPS = 1e-5
+PASSES = D_MODEL // (4 * P)
+ROWS = SEQ // P
+PAIR = 2
+PAIRS_PER_BATCH = ROWS // PAIR
+N_PAIRS = BATCH * PAIRS_PER_BATCH
+LOAD_AHEAD = 6
+FLOPS = 2 * BATCH * SEQ * D_MODEL * D_OUT
+
+
+def tile_multiheadattn_pb_t_kernel(tc, h_attn, Wo_words, Wo_scales, bo, x, gamma, beta, out):
+    nc = tc.nc
+    with ExitStack() as ctx:
+        const = ctx.enter_context(tc.tile_pool(name="const", bufs=1))
+        inputs = ctx.enter_context(tc.tile_pool(name="inputs", bufs=LOAD_AHEAD + 2))
+        sums = ctx.enter_context(tc.tile_pool(name="sums", bufs=3))
+        quant = ctx.enter_context(tc.tile_pool(name="quant", bufs=2))
+        small = ctx.enter_context(tc.tile_pool(name="small", bufs=2))
+        psum_t = ctx.enter_context(tc.psum_pool(name="psum_t", bufs=4))
+        psum_o = ctx.enter_context(tc.psum_pool(name="psum_o", bufs=3))
+        psum_s = ctx.enter_context(tc.psum_pool(name="psum_s", bufs=1))
+        ctx.enter_context(tc.manual_schedule())
+
+        h_view = h_attn.rearrange("b (p j) k -> b p j k", j=ROWS)
+        bo_view = bo.rearrange("b (p j) d -> b p j d", j=ROWS)
+        x_view = x.rearrange("b (p j) d -> b p j d", j=ROWS)
+        out_view = out.rearrange("b (p j) d -> b p j d", j=ROWS)
+        gamma_view = gamma.rearrange("(p j) d -> p j d", j=ROWS)
+        beta_view = beta.rearrange("(p j) d -> p j d", j=ROWS)
+
+        w_words = const.tile([P, PASSES, 2 * D_OUT], U8, align_bytes=64)
+        w_scales = const.tile([P, PASSES, D_OUT], U8, align_bytes=64)
+        gamma_sb = const.tile([P, ROWS, D_OUT], BF16)
+        beta_sb = const.tile([P, ROWS, D_OUT], BF16)
+        identity = const.tile([P, P], F32)
+        mean_matrix = const.tile([P, P], F32)
+        eps = const.tile([P, 1], F32)
+        table_warm = const.tile([P, 1], F32)
+
+        nc.vector.memset(w_scales[:].rearrange("p g n -> p (g n)").bitcast(I32), 0)
+        nc.vector.memset(eps[:], LN_EPS)
+        nc.vector.memset(mean_matrix[:], 1.0 / (SEQ * D_OUT))
+        make_identity(nc, identity[:])
+        nc.scalar.activation(out=table_warm[:], in_=eps[:], func=ACT.Sqrt)
+
+        h_tiles, bo_tiles, x_tiles = {}, {}, {}
+        grouped_tiles, code_tiles, scale_tiles, acc_tiles = {}, {}, {}, {}
+        o_tiles, stat_tiles, shift_tiles, mean_tiles, rstd_tiles, std_tiles = {}, {}, {}, {}, {}, {}
+
+        def rows_of(i):
+            k = i % PAIRS_PER_BATCH
+            return i // PAIRS_PER_BATCH, slice(PAIR * k, PAIR * (k + 1))
+
+        def load_pair(i):
+            b, rows = rows_of(i)
+            bo_pair = inputs.tile([P, PAIR, D_OUT], BF16)
+            x_pair = inputs.tile([P, PAIR, D_OUT], BF16)
+            h_pair = inputs.tile([P, PAIR, D_MODEL], BF16)
+            nc.sync.dma_start(out=bo_pair[:], in_=bo_view[b, :, rows, :])
+            nc.sync.dma_start(out=x_pair[:], in_=x_view[b, :, rows, :])
+            nc.sync.dma_start(out=h_pair[:], in_=h_view[b, :, rows, :])
+            bo_tiles[i], x_tiles[i], h_tiles[i] = bo_pair, x_pair, h_pair
+
+        def load_weights():
+            nc.sync.dma_start(
+                out=w_words[:].bitcast(I32), in_=Wo_words.rearrange("g p n -> p g n").bitcast(I32)
+            )
+            for quadrant in range(4):
+                nc.sync.dma_start(
+                    out=w_scales[32 * quadrant : 32 * quadrant + 4, :, :].bitcast(I32),
+                    in_=Wo_scales[:, 4 * quadrant : 4 * quadrant + 4, :].rearrange("g r n -> r g n").bitcast(I32),
+                )
+
+        def load_affine(k):
+            rows = slice(PAIR * k, PAIR * (k + 1))
+            nc.sync.dma_start(out=gamma_sb[:, rows, :], in_=gamma_view[:, rows, :])
+            nc.sync.dma_start(out=beta_sb[:, rows, :], in_=beta_view[:, rows, :])
+
+        def transpose_pair(i):
+            grouped = quant.tile([P, PAIR, PASSES, P, 4], BF16, align_bytes=64)
+            for a in range(PAIR):
+                h_words = h_tiles[i][:, a, :].bitcast(F32)
+                turned = psum_t.tile([P, PASSES, 2, P], F32)
+                for g in range(PASSES):
+                    for u in range(2):
+                        nc.tensor.transpose(
+                            turned[:, g, u, :], h_words[:, 256 * g + u : 256 * (g + 1) : 2], identity[:]
+                        )
+                nc.scalar.copy(out=grouped[:, a].bitcast(F32), in_=turned[:].rearrange("p g u r -> p g r u"))
+            grouped_tiles[i] = grouped
+
+        def quantise_pair(i):
+            codes = quant.tile([P, PAIR, PASSES, P], U32, align_bytes=64)
+            scales = quant.tile([P, PAIR, PASSES, P], U8, align_bytes=64)
+            nc.vector.quantize_mx(
+                out=codes[:].rearrange("p a g r -> p (a g r)").bitcast(FP8X4),
+                scales=scales[:].rearrange("p a g r -> p (a g r)"),
+                in_=grouped_tiles[i][:].rearrange("p a g r t -> p (a g r t)"),
+            )
+            code_tiles[i], scale_tiles[i] = codes, scales
+
+        def project_pair(i):
+            for a in range(PAIR):
+                acc = psum_o.tile([P, D_OUT], F32)
+                for g in range(PASSES):
+                    nc.tensor.matmul_mx(
+                        out=acc[:],
+                        lhsT=code_tiles[i][:, a, g, :].bitcast(FP8X4),
+                        lhsT_scale=scale_tiles[i][:, a, g, :],
+                        rhs=w_words[:, g, :].bitcast(FP4X4),
+                        rhs_scale=w_scales[:, g, :],
+                        start=(g == 0),
+                        stop=(g == PASSES - 1),
+                    )
+                acc_tiles[(i, a)] = acc
+
+        def add_bias_and_residual(i):
+            b, rows = rows_of(i)
+            if i % PAIRS_PER_BATCH == 0:
+                o_batch = sums.tile([P, ROWS, D_OUT], F32)
+                o_tiles[b] = o_batch
+            nc.vector.tensor_tensor(out=o_tiles[b][:, rows, :], in0=bo_tiles[i][:], in1=x_tiles[i][:], op=ALU.add)
+
+        def add_projection(i):
+            b, rows = rows_of(i)
+            if i % PAIRS_PER_BATCH == 0:
+                stat = small.tile([P, 2, ROWS], F32)
+                stat_tiles[b] = stat
+            stat = stat_tiles[b]
+            for a in range(PAIR):
+                j = PAIR * (i % PAIRS_PER_BATCH) + a
+                nc.vector.scalar_tensor_tensor(
+                    out=o_tiles[b][:, j, :],
+                    in0=acc_tiles[(i, a)][:],
+                    scalar=1.0,
+                    in1=o_tiles[b][:, j, :],
+                    op0=ALU.mult,
+                    op1=ALU.add,
+                    accum_out=stat[:, 0, j : j + 1],
+                )
+                if j == 0:
+                    part = psum_s.tile([P, 2 * ROWS], F32, tag="stat_ps")
+                    nc.tensor.matmul(out=part[:, 0:1], lhsT=mean_matrix[:], rhs=stat[:, 0, 0:1], start=True, stop=True)
+                    neg_shift = small.tile([P, 1], F32)
+                    nc.scalar.mul(out=neg_shift[:], in_=part[:, 0:1], mul=-float(ROWS))
+                    shift_tiles[b] = neg_shift
+            for a in range(PAIR):
+                j = PAIR * (i % PAIRS_PER_BATCH) + a
+                squares = small.tile([P, D_OUT], F32)
+                nc.scalar.activation(
+                    out=squares[:],
+                    in_=o_tiles[b][:, j, :],
+                    func=ACT.Square,
+                    bias=shift_tiles[b][:, 0:1],
+                    accum_out=stat[:, 1, j : j + 1],
+                )
+
+        def batch_mean_and_std(b):
+            total = psum_s.tile([P, 2 * ROWS], F32, tag="stat_ps")
+            nc.tensor.matmul(
+                out=total[:], lhsT=mean_matrix[:], rhs=stat_tiles[b][:].rearrange("p a j -> p (a j)"), start=True, stop=True
+            )
+            moments = small.tile([P, 2], F32)
+            nc.vector.tensor_reduce(
+                out=moments[:], in_=total[:].rearrange("p (a j) -> p a j", a=2), axis=mybir.AxisListType.X, op=ALU.add
+            )
+            offset = small.tile([P, 1], F32)
+            nc.vector.tensor_tensor(out=offset[:], in0=moments[:, 0:1], in1=shift_tiles[b][:], op=ALU.add)
+            neg_var = small.tile([P, 1], F32)
+            nc.vector.scalar_tensor_tensor(
+                out=neg_var[:], in0=offset[:], scalar=offset[:, 0:1], in1=moments[:, 1:2], op0=ALU.mult, op1=ALU.subtract
+            )
+            std = small.tile([P, 1], F32)
+            nc.scalar.activation(out=std[:], in_=neg_var[:], func=ACT.Sqrt, bias=eps[:, 0:1], scale=-1.0)
+            mean_tiles[b], std_tiles[b] = moments, std
+
+        def batch_rstd(b):
+            rstd = small.tile([P, 1], F32)
+            nc.vector.reciprocal(out=rstd[:], in_=std_tiles[b][:])
+            rstd_tiles[b] = rstd
+
+        def centre_and_gain(b, k):
+            rows = slice(PAIR * k, PAIR * (k + 1))
+            nc.vector.scalar_tensor_tensor(
+                out=o_tiles[b][:, rows, :],
+                in0=o_tiles[b][:, rows, :],
+                scalar=mean_tiles[b][:, 0:1],
+                in1=gamma_sb[:, rows, :],
+                op0=ALU.subtract,
+                op1=ALU.mult,
+            )
+
+        def scale_shift_store(b, k):
+            rows = slice(PAIR * k, PAIR * (k + 1))
+            nc.vector.scalar_tensor_tensor(
+                out=o_tiles[b][:, rows, :],
+                in0=o_tiles[b][:, rows, :],
+                scalar=rstd_tiles[b][:, 0:1],
+                in1=beta_sb[:, rows, :],
+                op0=ALU.mult,
+                op1=ALU.add,
+            )
+            nc.sync.dma_start(out=out_view[b, :, rows, :], in_=o_tiles[b][:, rows, :])
+
+        load_pair(0)
+        load_weights()
+        for i in range(1, LOAD_AHEAD):
+            load_pair(i)
+        load_affine(0)
+        add_bias_and_residual(0)
+        add_bias_and_residual(1)
+        transpose_pair(0)
+        transpose_pair(1)
+        quantise_pair(0)
+        project_pair(0)
+
+        for i in range(N_PAIRS):
+            b, k = i // PAIRS_PER_BATCH, i % PAIRS_PER_BATCH
+            if i + LOAD_AHEAD < N_PAIRS:
+                load_pair(i + LOAD_AHEAD)
+            if i + 1 < PAIRS_PER_BATCH:
+                load_affine(i + 1)
+            if i + 2 < N_PAIRS:
+                transpose_pair(i + 2)
+            if i + 1 < N_PAIRS:
+                quantise_pair(i + 1)
+                project_pair(i + 1)
+            add_projection(i)
+            if b > 0:
+                if k == 0:
+                    batch_rstd(b - 1)
+                centre_and_gain(b - 1, k)
+            if i + 2 < N_PAIRS:
+                add_bias_and_residual(i + 2)
+            if b > 0:
+                scale_shift_store(b - 1, k)
+            if k == PAIRS_PER_BATCH - 1:
+                batch_mean_and_std(b)
+
+        last = BATCH - 1
+        centre_and_gain(last, 0)
+        batch_rstd(last)
+        for k in range(1, PAIRS_PER_BATCH):
+            centre_and_gain(last, k)
+            scale_shift_store(last, k - 1)
+        scale_shift_store(last, PAIRS_PER_BATCH - 1)

@@ -21,7 +21,7 @@ ROWS = SEQ // P
 PAIR = 2
 PAIRS_PER_BATCH = ROWS // PAIR
 N_PAIRS = BATCH * PAIRS_PER_BATCH
-LOAD_AHEAD = 6
+LOAD_AHEAD = 5
 FLOPS = 2 * BATCH * SEQ * D_MODEL * D_OUT
 
 
@@ -29,13 +29,13 @@ def tile_multiheadattn_pb_t_kernel(tc, h_attn, Wo_words, Wo_scales, bo, x, gamma
     nc = tc.nc
     with ExitStack() as ctx:
         const = ctx.enter_context(tc.tile_pool(name="const", bufs=1))
-        inputs = ctx.enter_context(tc.tile_pool(name="inputs", bufs=LOAD_AHEAD + 2))
+        inputs = ctx.enter_context(tc.tile_pool(name="inputs", bufs=LOAD_AHEAD + 3))
         sums = ctx.enter_context(tc.tile_pool(name="sums", bufs=3))
         quant = ctx.enter_context(tc.tile_pool(name="quant", bufs=2))
         small = ctx.enter_context(tc.tile_pool(name="small", bufs=2))
-        psum_t = ctx.enter_context(tc.psum_pool(name="psum_t", bufs=4))
-        psum_o = ctx.enter_context(tc.psum_pool(name="psum_o", bufs=3))
-        psum_s = ctx.enter_context(tc.psum_pool(name="psum_s", bufs=1))
+        psum_g = ctx.enter_context(tc.psum_pool(name="psum_g", bufs=1))
+        psum_t = ctx.enter_context(tc.psum_pool(name="psum_t", bufs=2))
+        psum_o = ctx.enter_context(tc.psum_pool(name="psum_o", bufs=2))
         ctx.enter_context(tc.manual_schedule())
 
         h_view = h_attn.rearrange("b (p j) k -> b p j k", j=ROWS)
@@ -50,6 +50,8 @@ def tile_multiheadattn_pb_t_kernel(tc, h_attn, Wo_words, Wo_scales, bo, x, gamma
         gamma_sb = const.tile([P, ROWS, D_OUT], BF16)
         beta_sb = const.tile([P, ROWS, D_OUT], BF16)
         identity = const.tile([P, P], F32)
+        identity_bf16 = const.tile([P, P], BF16)
+        gamma_ps = psum_g.tile([P, ROWS, D_OUT], BF16)
         mean_matrix = const.tile([P, P], F32)
         eps = const.tile([P, 1], F32)
         table_warm = const.tile([P, 1], F32)
@@ -58,6 +60,7 @@ def tile_multiheadattn_pb_t_kernel(tc, h_attn, Wo_words, Wo_scales, bo, x, gamma
         nc.vector.memset(eps[:], LN_EPS)
         nc.vector.memset(mean_matrix[:], 1.0 / (SEQ * D_OUT))
         make_identity(nc, identity[:])
+        make_identity(nc, identity_bf16[:])
         nc.scalar.activation(out=table_warm[:], in_=eps[:], func=ACT.Sqrt)
 
         h_tiles, bo_tiles, x_tiles = {}, {}, {}
@@ -93,11 +96,15 @@ def tile_multiheadattn_pb_t_kernel(tc, h_attn, Wo_words, Wo_scales, bo, x, gamma
             nc.sync.dma_start(out=gamma_sb[:, rows, :], in_=gamma_view[:, rows, :])
             nc.sync.dma_start(out=beta_sb[:, rows, :], in_=beta_view[:, rows, :])
 
+        def park_gamma(k):
+            for j in range(PAIR * k, PAIR * (k + 1)):
+                nc.tensor.matmul(out=gamma_ps[:, j, :], lhsT=identity_bf16[:], rhs=gamma_sb[:, j, :], start=True, stop=True)
+
         def transpose_pair(i):
             grouped = quant.tile([P, PAIR, PASSES, P, 4], BF16, align_bytes=64)
             for a in range(PAIR):
                 h_words = h_tiles[i][:, a, :].bitcast(F32)
-                turned = psum_t.tile([P, PASSES, 2, P], F32)
+                turned = psum_t.tile([P, PASSES, 2, P], F32, tag="turned")
                 for g in range(PASSES):
                     for u in range(2):
                         nc.tensor.transpose(
@@ -136,7 +143,11 @@ def tile_multiheadattn_pb_t_kernel(tc, h_attn, Wo_words, Wo_scales, bo, x, gamma
             if i % PAIRS_PER_BATCH == 0:
                 o_batch = sums.tile([P, ROWS, D_OUT], F32)
                 o_tiles[b] = o_batch
-            nc.vector.tensor_tensor(out=o_tiles[b][:, rows, :], in0=bo_tiles[i][:], in1=x_tiles[i][:], op=ALU.add)
+            for a in range(PAIR):
+                j = PAIR * (i % PAIRS_PER_BATCH) + a
+                nc.gpsimd.tensor_tensor(
+                    out=o_tiles[b][:, j, :], in0=bo_tiles[i][:, a, :], in1=x_tiles[i][:, a, :], op=ALU.add
+                )
 
         def add_projection(i):
             b, rows = rows_of(i)
@@ -156,7 +167,7 @@ def tile_multiheadattn_pb_t_kernel(tc, h_attn, Wo_words, Wo_scales, bo, x, gamma
                     accum_out=stat[:, 0, j : j + 1],
                 )
                 if j == 0:
-                    part = psum_s.tile([P, 2 * ROWS], F32, tag="stat_ps")
+                    part = psum_t.tile([P, 2 * ROWS], F32, tag="turned")
                     nc.tensor.matmul(out=part[:, 0:1], lhsT=mean_matrix[:], rhs=stat[:, 0, 0:1], start=True, stop=True)
                     neg_shift = small.tile([P, 1], F32)
                     nc.scalar.mul(out=neg_shift[:], in_=part[:, 0:1], mul=-float(ROWS))
@@ -173,7 +184,7 @@ def tile_multiheadattn_pb_t_kernel(tc, h_attn, Wo_words, Wo_scales, bo, x, gamma
                 )
 
         def batch_mean_and_std(b):
-            total = psum_s.tile([P, 2 * ROWS], F32, tag="stat_ps")
+            total = psum_t.tile([P, 2 * ROWS], F32, tag="turned")
             nc.tensor.matmul(
                 out=total[:], lhsT=mean_matrix[:], rhs=stat_tiles[b][:].rearrange("p a j -> p (a j)"), start=True, stop=True
             )
@@ -202,7 +213,7 @@ def tile_multiheadattn_pb_t_kernel(tc, h_attn, Wo_words, Wo_scales, bo, x, gamma
                 out=o_tiles[b][:, rows, :],
                 in0=o_tiles[b][:, rows, :],
                 scalar=mean_tiles[b][:, 0:1],
-                in1=gamma_sb[:, rows, :],
+                in1=gamma_ps[:, rows, :],
                 op0=ALU.subtract,
                 op1=ALU.mult,
             )
@@ -231,8 +242,7 @@ def tile_multiheadattn_pb_t_kernel(tc, h_attn, Wo_words, Wo_scales, bo, x, gamma
         quantise_pair(0)
         project_pair(0)
 
-        for i in range(N_PAIRS):
-            b, k = i // PAIRS_PER_BATCH, i % PAIRS_PER_BATCH
+        for i in range(N_PAIRS + PAIRS_PER_BATCH + 1):
             if i + LOAD_AHEAD < N_PAIRS:
                 load_pair(i + LOAD_AHEAD)
             if i + 1 < PAIRS_PER_BATCH:
@@ -242,22 +252,18 @@ def tile_multiheadattn_pb_t_kernel(tc, h_attn, Wo_words, Wo_scales, bo, x, gamma
             if i + 1 < N_PAIRS:
                 quantise_pair(i + 1)
                 project_pair(i + 1)
-            add_projection(i)
-            if b > 0:
-                if k == 0:
-                    batch_rstd(b - 1)
-                centre_and_gain(b - 1, k)
+            if 0 <= i - (PAIRS_PER_BATCH - 1) < PAIRS_PER_BATCH:
+                park_gamma(i - (PAIRS_PER_BATCH - 1))
+            if i < N_PAIRS:
+                add_projection(i)
+            centred = i - PAIRS_PER_BATCH
+            if 0 <= centred < N_PAIRS:
+                centre_and_gain(centred // PAIRS_PER_BATCH, centred % PAIRS_PER_BATCH)
+                if centred % PAIRS_PER_BATCH == 0:
+                    batch_rstd(centred // PAIRS_PER_BATCH)
             if i + 2 < N_PAIRS:
                 add_bias_and_residual(i + 2)
-            if b > 0:
-                scale_shift_store(b - 1, k)
-            if k == PAIRS_PER_BATCH - 1:
-                batch_mean_and_std(b)
-
-        last = BATCH - 1
-        centre_and_gain(last, 0)
-        batch_rstd(last)
-        for k in range(1, PAIRS_PER_BATCH):
-            centre_and_gain(last, k)
-            scale_shift_store(last, k - 1)
-        scale_shift_store(last, PAIRS_PER_BATCH - 1)
+            if 0 <= centred - 1:
+                scale_shift_store((centred - 1) // PAIRS_PER_BATCH, (centred - 1) % PAIRS_PER_BATCH)
+            if i < N_PAIRS and i % PAIRS_PER_BATCH == PAIRS_PER_BATCH - 1:
+                batch_mean_and_std(i // PAIRS_PER_BATCH)

@@ -36,7 +36,6 @@ def tile_multiheadattn_pb_t_kernel(tc, h_attn, Wo_words, Wo_scales, bo, x, gamma
         psum_g = ctx.enter_context(tc.psum_pool(name="psum_g", bufs=1))
         psum_t = ctx.enter_context(tc.psum_pool(name="psum_t", bufs=2))
         psum_o = ctx.enter_context(tc.psum_pool(name="psum_o", bufs=2))
-        ctx.enter_context(tc.manual_schedule())
 
         h_view = h_attn.rearrange("b (p j) k -> b p j k", j=ROWS)
         bo_view = bo.rearrange("b (p j) d -> b p j d", j=ROWS)

@@ -142,9 +142,10 @@ def tile_multiheadattn_pb_t_kernel(tc, h_attn, Wo_words, Wo_scales, bo, x, gamma
             if i % PAIRS_PER_BATCH == 0:
                 o_batch = sums.tile([P, ROWS, D_OUT], F32)
                 o_tiles[b] = o_batch
+            adder = nc.vector if b == 0 else nc.gpsimd
             for a in range(PAIR):
                 j = PAIR * (i % PAIRS_PER_BATCH) + a
-                nc.gpsimd.tensor_tensor(
+                adder.tensor_tensor(
                     out=o_tiles[b][:, j, :], in0=bo_tiles[i][:, a, :], in1=x_tiles[i][:, a, :], op=ALU.add
                 )
 

@@ -22,6 +22,7 @@ PAIR = 2
 PAIRS_PER_BATCH = ROWS // PAIR
 N_PAIRS = BATCH * PAIRS_PER_BATCH
 LOAD_AHEAD = 5
+GPSIMD_PIECE = 256
 FLOPS = 2 * BATCH * SEQ * D_MODEL * D_OUT
 
 
@@ -142,12 +143,16 @@ def tile_multiheadattn_pb_t_kernel(tc, h_attn, Wo_words, Wo_scales, bo, x, gamma
             if i % PAIRS_PER_BATCH == 0:
                 o_batch = sums.tile([P, ROWS, D_OUT], F32)
                 o_tiles[b] = o_batch
-            adder = nc.vector if b == 0 else nc.gpsimd
+            adder, width = (nc.vector, D_OUT) if b == 0 else (nc.gpsimd, GPSIMD_PIECE)
             for a in range(PAIR):
                 j = PAIR * (i % PAIRS_PER_BATCH) + a
-                adder.tensor_tensor(
-                    out=o_tiles[b][:, j, :], in0=bo_tiles[i][:, a, :], in1=x_tiles[i][:, a, :], op=ALU.add
-                )
+                for c in range(0, D_OUT, width):
+                    adder.tensor_tensor(
+                        out=o_tiles[b][:, j, c : c + width],
+                        in0=bo_tiles[i][:, a, c : c + width],
+                        in1=x_tiles[i][:, a, c : c + width],
+                        op=ALU.add,
+                    )
 
         def add_projection(i):
             b, rows = rows_of(i)

@@ -23,6 +23,7 @@ PAIRS_PER_BATCH = ROWS // PAIR
 N_PAIRS = BATCH * PAIRS_PER_BATCH
 LOAD_AHEAD = 5
 GPSIMD_PIECE = 256
+TENSOR_PAIRS = (1, 3)
 FLOPS = 2 * BATCH * SEQ * D_MODEL * D_OUT
 
 
@@ -34,9 +35,9 @@ def tile_multiheadattn_pb_t_kernel(tc, h_attn, Wo_words, Wo_scales, bo, x, gamma
         sums = ctx.enter_context(tc.tile_pool(name="sums", bufs=3))
         quant = ctx.enter_context(tc.tile_pool(name="quant", bufs=2))
         small = ctx.enter_context(tc.tile_pool(name="small", bufs=2))
-        psum_g = ctx.enter_context(tc.psum_pool(name="psum_g", bufs=1))
-        psum_t = ctx.enter_context(tc.psum_pool(name="psum_t", bufs=2))
-        psum_o = ctx.enter_context(tc.psum_pool(name="psum_o", bufs=2))
+        psum_c = ctx.enter_context(tc.psum_pool(name="psum_c", bufs=2))
+        psum_t = ctx.enter_context(tc.psum_pool(name="psum_t", bufs=3))
+        psum_o = ctx.enter_context(tc.psum_pool(name="psum_o", bufs=3))
 
         h_view = h_attn.rearrange("b (p j) k -> b p j k", j=ROWS)
         bo_view = bo.rearrange("b (p j) d -> b p j d", j=ROWS)
@@ -51,7 +52,6 @@ def tile_multiheadattn_pb_t_kernel(tc, h_attn, Wo_words, Wo_scales, bo, x, gamma
         beta_sb = const.tile([P, ROWS, D_OUT], BF16)
         identity = const.tile([P, P], F32)
         identity_bf16 = const.tile([P, P], BF16)
-        gamma_ps = psum_g.tile([P, ROWS, D_OUT], BF16)
         mean_matrix = const.tile([P, P], F32)
         eps = const.tile([P, 1], F32)
         table_warm = const.tile([P, 1], F32)
@@ -95,10 +95,6 @@ def tile_multiheadattn_pb_t_kernel(tc, h_attn, Wo_words, Wo_scales, bo, x, gamma
             rows = slice(PAIR * k, PAIR * (k + 1))
             nc.sync.dma_start(out=gamma_sb[:, rows, :], in_=gamma_view[:, rows, :])
             nc.sync.dma_start(out=beta_sb[:, rows, :], in_=beta_view[:, rows, :])
-
-        def park_gamma(k):
-            for j in range(PAIR * k, PAIR * (k + 1)):
-                nc.tensor.matmul(out=gamma_ps[:, j, :], lhsT=identity_bf16[:], rhs=gamma_sb[:, j, :], start=True, stop=True)
 
         def transpose_pair(i):
             grouped = quant.tile([P, PAIR, PASSES, P, 4], BF16, align_bytes=64)
@@ -146,6 +142,12 @@ def tile_multiheadattn_pb_t_kernel(tc, h_attn, Wo_words, Wo_scales, bo, x, gamma
             adder, width = (nc.vector, D_OUT) if b == 0 else (nc.gpsimd, GPSIMD_PIECE)
             for a in range(PAIR):
                 j = PAIR * (i % PAIRS_PER_BATCH) + a
+                if b > 0 and i % PAIRS_PER_BATCH in TENSOR_PAIRS:
+                    both = psum_c.tile([P, D_OUT], F32)
+                    nc.tensor.matmul(out=both[:], lhsT=identity_bf16[:], rhs=bo_tiles[i][:, a, :], start=True, stop=False)
+                    nc.tensor.matmul(out=both[:], lhsT=identity_bf16[:], rhs=x_tiles[i][:, a, :], start=False, stop=True)
+                    nc.scalar.copy(out=o_tiles[b][:, j, :], in_=both[:])
+                    continue
                 for c in range(0, D_OUT, width):
                     adder.tensor_tensor(
                         out=o_tiles[b][:, j, c : c + width],
@@ -218,7 +220,7 @@ def tile_multiheadattn_pb_t_kernel(tc, h_attn, Wo_words, Wo_scales, bo, x, gamma
                 out=o_tiles[b][:, rows, :],
                 in0=o_tiles[b][:, rows, :],
                 scalar=mean_tiles[b][:, 0:1],
-                in1=gamma_ps[:, rows, :],
+                in1=gamma_sb[:, rows, :],
                 op0=ALU.subtract,
                 op1=ALU.mult,
             )
@@ -257,8 +259,6 @@ def tile_multiheadattn_pb_t_kernel(tc, h_attn, Wo_words, Wo_scales, bo, x, gamma
             if i + 1 < N_PAIRS:
                 quantise_pair(i + 1)
                 project_pair(i + 1)
-            if 0 <= i - (PAIRS_PER_BATCH - 1) < PAIRS_PER_BATCH:
-                park_gamma(i - (PAIRS_PER_BATCH - 1))
             if i < N_PAIRS:
                 add_projection(i)
             centred = i - PAIRS_PER_BATCH

@@ -237,6 +237,7 @@ def tile_multiheadattn_pb_t_kernel(tc, h_attn, Wo_words, Wo_scales, bo, x, gamma
             )
             nc.sync.dma_start(out=out_view[b, :, rows, :], in_=o_tiles[b][:, rows, :])
 
+        ctx.enter_context(tc.manual_schedule(engines={mybir.EngineType.PE}))
         load_pair(0)
         load_weights()
         for i in range(1, LOAD_AHEAD):

@@ -214,8 +214,8 @@ def tile_multiheadattn_pb_t_kernel(tc, h_attn, Wo_words, Wo_scales, bo, x, gamma
             nc.vector.reciprocal(out=rstd[:], in_=std_tiles[b][:])
             rstd_tiles[b] = rstd
 
-        def centre_and_gain(b, k):
-            rows = slice(PAIR * k, PAIR * (k + 1))
+        def centre_and_gain(b, k, pairs=1):
+            rows = slice(PAIR * k, PAIR * (k + pairs))
             nc.vector.scalar_tensor_tensor(
                 out=o_tiles[b][:, rows, :],
                 in0=o_tiles[b][:, rows, :],
@@ -225,8 +225,8 @@ def tile_multiheadattn_pb_t_kernel(tc, h_attn, Wo_words, Wo_scales, bo, x, gamma
                 op1=ALU.mult,
             )
 
-        def scale_shift_store(b, k):
-            rows = slice(PAIR * k, PAIR * (k + 1))
+        def scale_shift_store(b, k, pairs=1):
+            rows = slice(PAIR * k, PAIR * (k + pairs))
             nc.vector.scalar_tensor_tensor(
                 out=o_tiles[b][:, rows, :],
                 in0=o_tiles[b][:, rows, :],
@@ -263,13 +263,18 @@ def tile_multiheadattn_pb_t_kernel(tc, h_attn, Wo_words, Wo_scales, bo, x, gamma
             if i < N_PAIRS:
                 add_projection(i)
             centred = i - PAIRS_PER_BATCH
-            if 0 <= centred < N_PAIRS:
+            wide = 0 <= centred < N_PAIRS - PAIRS_PER_BATCH
+            if wide and centred % 2 == 0:
+                centre_and_gain(centred // PAIRS_PER_BATCH, centred % PAIRS_PER_BATCH, pairs=2)
+            if N_PAIRS - PAIRS_PER_BATCH <= centred < N_PAIRS:
                 centre_and_gain(centred // PAIRS_PER_BATCH, centred % PAIRS_PER_BATCH)
-                if centred % PAIRS_PER_BATCH == 0:
-                    batch_rstd(centred // PAIRS_PER_BATCH)
+            if 0 <= centred < N_PAIRS and centred % PAIRS_PER_BATCH == 0:
+                batch_rstd(centred // PAIRS_PER_BATCH)
             if i + 2 < N_PAIRS:
                 add_bias_and_residual(i + 2)
-            if 0 <= centred - 1:
+            if wide and centred % 2 == 1:
+                scale_shift_store(centred // PAIRS_PER_BATCH, centred % PAIRS_PER_BATCH - 1, pairs=2)
+            if N_PAIRS - PAIRS_PER_BATCH <= centred - 1:
                 scale_shift_store((centred - 1) // PAIRS_PER_BATCH, (centred - 1) % PAIRS_PER_BATCH)
             if i < N_PAIRS and i % PAIRS_PER_BATCH == PAIRS_PER_BATCH - 1:
                 batch_mean_and_std(i // PAIRS_PER_BATCH)

from contextlib import ExitStack

import concourse.mybir as mybir
from concourse.masks import make_identity

F32 = mybir.dt.float32
BF16 = mybir.dt.bfloat16
I32 = mybir.dt.int32
U32 = mybir.dt.uint32
U8 = mybir.dt.uint8
FP8X4 = mybir.dt.float8_e4m3fn_x4
FP4X4 = mybir.dt.float4_e2m1fn_x4
ALU = mybir.AluOpType
ACT = mybir.ActivationFunctionType

P = 128
BATCH, SEQ, D_MODEL, D_OUT = 4, 1024, 1024, 512
LN_EPS = 1e-5
PASSES = D_MODEL // (4 * P)
ROWS = SEQ // P
PAIR = 2
PAIRS_PER_BATCH = ROWS // PAIR
N_PAIRS = BATCH * PAIRS_PER_BATCH
LOAD_AHEAD = 5
GPSIMD_PIECE = 256
TENSOR_PAIRS = (1, 3)
FLOPS = 2 * BATCH * SEQ * D_MODEL * D_OUT


def tile_multiheadattn_pb_t_kernel(tc, h_attn, Wo_words, Wo_scales, bo, x, gamma, beta, out):
    nc = tc.nc
    with ExitStack() as ctx:
        const = ctx.enter_context(tc.tile_pool(name="const", bufs=1))
        inputs = ctx.enter_context(tc.tile_pool(name="inputs", bufs=LOAD_AHEAD + 3))
        sums = ctx.enter_context(tc.tile_pool(name="sums", bufs=3))
        quant = ctx.enter_context(tc.tile_pool(name="quant", bufs=2))
        small = ctx.enter_context(tc.tile_pool(name="small", bufs=2))
        psum_c = ctx.enter_context(tc.psum_pool(name="psum_c", bufs=2))
        psum_t = ctx.enter_context(tc.psum_pool(name="psum_t", bufs=3))
        psum_o = ctx.enter_context(tc.psum_pool(name="psum_o", bufs=3))

        h_view = h_attn.rearrange("b (p j) k -> b p j k", j=ROWS)
        bo_view = bo.rearrange("b (p j) d -> b p j d", j=ROWS)
        x_view = x.rearrange("b (p j) d -> b p j d", j=ROWS)
        out_view = out.rearrange("b (p j) d -> b p j d", j=ROWS)
        gamma_view = gamma.rearrange("(p j) d -> p j d", j=ROWS)
        beta_view = beta.rearrange("(p j) d -> p j d", j=ROWS)

        w_words = const.tile([P, PASSES, 2 * D_OUT], U8, align_bytes=64)
        w_scales = const.tile([P, PASSES, D_OUT], U8, align_bytes=64)
        gamma_sb = const.tile([P, ROWS, D_OUT], BF16)
        beta_sb = const.tile([P, ROWS, D_OUT], BF16)
        identity = const.tile([P, P], F32)
        identity_bf16 = const.tile([P, P], BF16)
        mean_matrix = const.tile([P, P], F32)
        eps = const.tile([P, 1], F32)
        table_warm = const.tile([P, 1], F32)

        nc.vector.memset(w_scales[:].rearrange("p g n -> p (g n)").bitcast(I32), 0)
        nc.vector.memset(eps[:], LN_EPS)
        nc.vector.memset(mean_matrix[:], 1.0 / (SEQ * D_OUT))
        make_identity(nc, identity[:])
        make_identity(nc, identity_bf16[:])
        nc.scalar.activation(out=table_warm[:], in_=eps[:], func=ACT.Sqrt)

        h_tiles, bo_tiles, x_tiles = {}, {}, {}
        grouped_tiles, code_tiles, scale_tiles, acc_tiles = {}, {}, {}, {}
        o_tiles, stat_tiles, shift_tiles, mean_tiles, rstd_tiles, std_tiles = {}, {}, {}, {}, {}, {}

        def rows_of(i):
            k = i % PAIRS_PER_BATCH
            return i // PAIRS_PER_BATCH, slice(PAIR * k, PAIR * (k + 1))

        def load_pair(i):
            b, rows = rows_of(i)
            bo_pair = inputs.tile([P, PAIR, D_OUT], BF16)
            x_pair = inputs.tile([P, PAIR, D_OUT], BF16)
            h_pair = inputs.tile([P, PAIR, D_MODEL], BF16)
            nc.sync.dma_start(out=bo_pair[:], in_=bo_view[b, :, rows, :])
            nc.sync.dma_start(out=x_pair[:], in_=x_view[b, :, rows, :])
            nc.sync.dma_start(out=h_pair[:], in_=h_view[b, :, rows, :])
            bo_tiles[i], x_tiles[i], h_tiles[i] = bo_pair, x_pair, h_pair

        def load_weights():
            nc.sync.dma_start(
                out=w_words[:].bitcast(I32), in_=Wo_words.rearrange("g p n -> p g n").bitcast(I32)
            )
            for quadrant in range(4):
                nc.sync.dma_start(
                    out=w_scales[32 * quadrant : 32 * quadrant + 4, :, :].bitcast(I32),
                    in_=Wo_scales[:, 4 * quadrant : 4 * quadrant + 4, :].rearrange("g r n -> r g n").bitcast(I32),
                )

        def load_affine(k):
            rows = slice(PAIR * k, PAIR * (k + 1))
            nc.sync.dma_start(out=gamma_sb[:, rows, :], in_=gamma_view[:, rows, :])
            nc.sync.dma_start(out=beta_sb[:, rows, :], in_=beta_view[:, rows, :])

        def transpose_pair(i):
            grouped = quant.tile([P, PAIR, PASSES, P, 4], BF16, align_bytes=64)
            for a in range(PAIR):
                h_words = h_tiles[i][:, a, :].bitcast(F32)
                turned = psum_t.tile([P, PASSES, 2, P], F32, tag="turned")
                for g in range(PASSES):
                    for u in range(2):
                        nc.tensor.transpose(
                            turned[:, g, u, :], h_words[:, 256 * g + u : 256 * (g + 1) : 2], identity[:]
                        )
                nc.scalar.copy(out=grouped[:, a].bitcast(F32), in_=turned[:].rearrange("p g u r -> p g r u"))
            grouped_tiles[i] = grouped

        def quantise_pair(i):
            codes = quant.tile([P, PAIR, PASSES, P], U32, align_bytes=64)
            scales = quant.tile([P, PAIR, PASSES, P], U8, align_bytes=64)
            nc.vector.quantize_mx(
                out=codes[:].rearrange("p a g r -> p (a g r)").bitcast(FP8X4),
                scales=scales[:].rearrange("p a g r -> p (a g r)"),
                in_=grouped_tiles[i][:].rearrange("p a g r t -> p (a g r t)"),
            )
            code_tiles[i], scale_tiles[i] = codes, scales

        def project_pair(i):
            for a in range(PAIR):
                acc = psum_o.tile([P, D_OUT], F32)
                for g in range(PASSES):
                    nc.tensor.matmul_mx(
                        out=acc[:],
                        lhsT=code_tiles[i][:, a, g, :].bitcast(FP8X4),
                        lhsT_scale=scale_tiles[i][:, a, g, :],
                        rhs=w_words[:, g, :].bitcast(FP4X4),
                        rhs_scale=w_scales[:, g, :],
                        start=(g == 0),
                        stop=(g == PASSES - 1),
                    )
                acc_tiles[(i, a)] = acc

        def add_bias_and_residual(i):
            b, rows = rows_of(i)
            if i % PAIRS_PER_BATCH == 0:
                o_batch = sums.tile([P, ROWS, D_OUT], F32)
                o_tiles[b] = o_batch
            adder, width = (nc.vector, D_OUT) if b == 0 else (nc.gpsimd, GPSIMD_PIECE)
            for a in range(PAIR):
                j = PAIR * (i % PAIRS_PER_BATCH) + a
                if b > 0 and i % PAIRS_PER_BATCH in TENSOR_PAIRS:
                    both = psum_c.tile([P, D_OUT], F32)
                    nc.tensor.matmul(out=both[:], lhsT=identity_bf16[:], rhs=bo_tiles[i][:, a, :], start=True, stop=False)
                    nc.tensor.matmul(out=both[:], lhsT=identity_bf16[:], rhs=x_tiles[i][:, a, :], start=False, stop=True)
                    nc.scalar.copy(out=o_tiles[b][:, j, :], in_=both[:])
                    continue
                for c in range(0, D_OUT, width):
                    adder.tensor_tensor(
                        out=o_tiles[b][:, j, c : c + width],
                        in0=bo_tiles[i][:, a, c : c + width],
                        in1=x_tiles[i][:, a, c : c + width],
                        op=ALU.add,
                    )

        def add_projection(i):
            b, rows = rows_of(i)
            if i % PAIRS_PER_BATCH == 0:
                stat = small.tile([P, 2, ROWS], F32)
                stat_tiles[b] = stat
            stat = stat_tiles[b]
            for a in range(PAIR):
                j = PAIR * (i % PAIRS_PER_BATCH) + a
                nc.vector.scalar_tensor_tensor(
                    out=o_tiles[b][:, j, :],
                    in0=acc_tiles[(i, a)][:],
                    scalar=1.0,
                    in1=o_tiles[b][:, j, :],
                    op0=ALU.mult,
                    op1=ALU.add,
                    accum_out=stat[:, 0, j : j + 1],
                )
                if j == 0:
                    part = psum_t.tile([P, 2 * ROWS], F32, tag="turned")
                    nc.tensor.matmul(out=part[:, 0:1], lhsT=mean_matrix[:], rhs=stat[:, 0, 0:1], start=True, stop=True)
                    neg_shift = small.tile([P, 1], F32)
                    nc.scalar.mul(out=neg_shift[:], in_=part[:, 0:1], mul=-float(ROWS))
                    shift_tiles[b] = neg_shift
            for a in range(PAIR):
                j = PAIR * (i % PAIRS_PER_BATCH) + a
                squares = small.tile([P, D_OUT], F32)
                nc.scalar.activation(
                    out=squares[:],
                    in_=o_tiles[b][:, j, :],
                    func=ACT.Square,
                    bias=shift_tiles[b][:, 0:1],
                    accum_out=stat[:, 1, j : j + 1],
                )

        def batch_mean_and_std(b):
            total = psum_t.tile([P, 2 * ROWS], F32, tag="turned")
            nc.tensor.matmul(
                out=total[:], lhsT=mean_matrix[:], rhs=stat_tiles[b][:].rearrange("p a j -> p (a j)"), start=True, stop=True
            )
            moments = small.tile([P, 2], F32)
            nc.vector.tensor_reduce(
                out=moments[:], in_=total[:].rearrange("p (a j) -> p a j", a=2), axis=mybir.AxisListType.X, op=ALU.add
            )
            offset = small.tile([P, 1], F32)
            nc.vector.tensor_tensor(out=offset[:], in0=moments[:, 0:1], in1=shift_tiles[b][:], op=ALU.add)
            neg_var = small.tile([P, 1], F32)
            nc.vector.scalar_tensor_tensor(
                out=neg_var[:], in0=offset[:], scalar=offset[:, 0:1], in1=moments[:, 1:2], op0=ALU.mult, op1=ALU.subtract
            )
            std = small.tile([P, 1], F32)
            nc.scalar.activation(out=std[:], in_=neg_var[:], func=ACT.Sqrt, bias=eps[:, 0:1], scale=-1.0)
            mean_tiles[b], std_tiles[b] = moments, std

        def batch_rstd(b):
            rstd = small.tile([P, 1], F32)
            nc.vector.reciprocal(out=rstd[:], in_=std_tiles[b][:])
            rstd_tiles[b] = rstd

        def centre_and_gain(b, k, pairs=1):
            rows = slice(PAIR * k, PAIR * (k + pairs))
            nc.vector.scalar_tensor_tensor(
                out=o_tiles[b][:, rows, :],
                in0=o_tiles[b][:, rows, :],
                scalar=mean_tiles[b][:, 0:1],
                in1=gamma_sb[:, rows, :],
                op0=ALU.subtract,
                op1=ALU.mult,
            )

        def scale_shift_store(b, k, pairs=1):
            rows = slice(PAIR * k, PAIR * (k + pairs))
            nc.vector.scalar_tensor_tensor(
                out=o_tiles[b][:, rows, :],
                in0=o_tiles[b][:, rows, :],
                scalar=rstd_tiles[b][:, 0:1],
                in1=beta_sb[:, rows, :],
                op0=ALU.mult,
                op1=ALU.add,
            )
            nc.sync.dma_start(out=out_view[b, :, rows, :], in_=o_tiles[b][:, rows, :])

        ctx.enter_context(tc.manual_schedule(engines={mybir.EngineType.PE}))
        load_pair(0)
        load_weights()
        for i in range(1, LOAD_AHEAD):
            load_pair(i)
        load_affine(0)
        add_bias_and_residual(0)
        add_bias_and_residual(1)
        transpose_pair(0)
        transpose_pair(1)
        quantise_pair(0)
        project_pair(0)

        for i in range(N_PAIRS + PAIRS_PER_BATCH + 1):
            if i + LOAD_AHEAD < N_PAIRS:
                load_pair(i + LOAD_AHEAD)
            if i + 1 < PAIRS_PER_BATCH:
                load_affine(i + 1)
            if i + 2 < N_PAIRS:
                transpose_pair(i + 2)
            if i + 1 < N_PAIRS:
                quantise_pair(i + 1)
                project_pair(i + 1)
            if i < N_PAIRS:
                add_projection(i)
            centred = i - PAIRS_PER_BATCH
            wide = 0 <= centred < N_PAIRS - PAIRS_PER_BATCH
            if wide and centred % 2 == 0:
                centre_and_gain(centred // PAIRS_PER_BATCH, centred % PAIRS_PER_BATCH, pairs=2)
            if N_PAIRS - PAIRS_PER_BATCH <= centred < N_PAIRS:
                centre_and_gain(centred // PAIRS_PER_BATCH, centred % PAIRS_PER_BATCH)
            if 0 <= centred < N_PAIRS and centred % PAIRS_PER_BATCH == 0:
                batch_rstd(centred // PAIRS_PER_BATCH)
            if i + 2 < N_PAIRS:
                add_bias_and_residual(i + 2)
            if wide and centred % 2 == 1:
                scale_shift_store(centred // PAIRS_PER_BATCH, centred % PAIRS_PER_BATCH - 1, pairs=2)
            if N_PAIRS - PAIRS_PER_BATCH <= centred - 1:
                scale_shift_store((centred - 1) // PAIRS_PER_BATCH, (centred - 1) % PAIRS_PER_BATCH)
            if i < N_PAIRS and i % PAIRS_PER_BATCH == PAIRS_PER_BATCH - 1:
                batch_mean_and_std(i // PAIRS_PER_BATCH)
